import numpy as np
import ml_dtypes


def mxq(x, axis, fmt="e4m3"):
    dtype, down = {"e4m3": (ml_dtypes.float8_e4m3fn, 7), "e5m2": (ml_dtypes.float8_e5m2, 14)}[fmt]
    v = np.moveaxis(np.asarray(x, np.float32).astype(ml_dtypes.bfloat16).astype(np.float64), axis, -1)
    blocks = v.reshape(v.shape[:-1] + (-1, 32))
    amax = np.abs(blocks).max(-1, keepdims=True)
    byte = np.maximum(np.where(amax > 0, np.frexp(amax)[1] - 1 + 127, 0) - down, 1)
    scale = np.exp2(byte - 127.0)
    codes = (blocks / scale).astype(np.float32).astype(dtype).astype(np.float64)
    return np.moveaxis((codes * scale).reshape(v.shape), -1, axis)


WIDE = False


def mx_kscale(k):
    if not WIDE:
        return np.ones(k)
    levels = np.array([10, -10, 5, -5, 0])
    a = np.random.permutation(np.resize(levels, k // 512 * 4)).reshape(k // 512, 4)
    idx = np.arange(k)
    return np.exp2(a[idx // 512, idx % 128 // 32])


BF16 = ml_dtypes.bfloat16


def bf(x):
    return np.asarray(x, np.float32).astype(BF16)


def f64(x):
    return np.asarray(x).astype(np.float64)


B, D0, D1, D2, D3, D4 = 8192, 512, 512, 512, 1024, 256
DENSITY = 0.02


def setup_inputs():
    s, t = mx_kscale(D0), mx_kscale(D1)
    bound0 = np.sqrt(3.0 / (DENSITY * D0))
    bound1 = np.sqrt(6.0 / (DENSITY * D1))
    return {"x": bf(np.random.standard_normal((B, D0)) * s),
            "W0": bf(np.random.uniform(-bound0, bound0, (D1, D0)) / s[None, :] * t[:, None]),
            "b0": bf(np.random.standard_normal(D1) * 0.3 * t),
            "m0": bf(np.random.uniform(size=(D1, D0)) < DENSITY),
            "W1": bf(np.random.uniform(-bound1, bound1, (D2, D1)) / t[None, :]),
            "b1": bf(np.random.standard_normal(D2) * 0.3),
            "m1": bf(np.random.uniform(size=(D2, D1)) < DENSITY)}


def reference(x, W0, b0, m0, W1, b1, m1):
    h = f64(x).reshape(x.shape[0], -1)
    w0 = f64(W0) * f64(m0)
    pre0 = (mxq(h, 1, "e4m3") @ mxq(w0, 1, "e4m3").T) + f64(b0)
    h0 = np.maximum(pre0, 0.0)
    w1 = f64(W1) * f64(m1)
    pre1 = (mxq(h0, 1, "e4m3") @ mxq(w1, 1, "e4m3").T) + f64(b1)
    return np.maximum(pre1, 0.0)

@@ -1,0 +1,198 @@
+from contextlib import ExitStack
+
+import concourse.mybir as mybir
+from concourse.masks import make_identity
+
+F32 = mybir.dt.float32
+BF16 = mybir.dt.bfloat16
+U32 = mybir.dt.uint32
+U8 = mybir.dt.uint8
+FP8X4 = mybir.dt.float8_e4m3fn_x4
+ALU = mybir.AluOpType
+ACT = mybir.ActivationFunctionType
+
+P = 128
+PACK = 4
+WIDTH = P * PACK
+TOKENS = 8192
+GROUPS = TOKENS // WIDTH
+HALF = WIDTH // 2
+FLOAT32_MAX = 3.4028234663852886e38
+
+FLOPS = 2 * 2 * TOKENS * WIDTH * WIDTH
+
+
+def tile_patchedsparsenetwork_pa_t_kernel(tc, x, W0, b0, m0, W1, b1, m1, out):
+    nc = tc.nc
+    x_groups = x.rearrange("(g p r) k -> g p (r k)", p=P, r=PACK)
+    out_groups = out.rearrange("(g p r) d -> g p r d", p=P, r=PACK)
+
+    with ExitStack() as ctx:
+        consts = ctx.enter_context(tc.tile_pool(name="consts", bufs=1))
+        x_pool = ctx.enter_context(tc.tile_pool(name="x_pool", bufs=GROUPS))
+        grouped_pool = ctx.enter_context(tc.tile_pool(name="grouped_pool", bufs=3))
+        mx_pool = ctx.enter_context(tc.tile_pool(name="mx_pool", bufs=2))
+        out_pool = ctx.enter_context(tc.tile_pool(name="out_pool", bufs=4))
+        psum_t = ctx.enter_context(tc.psum_pool(name="psum_t", bufs=2))
+        psum_1 = ctx.enter_context(tc.psum_pool(name="psum_1", bufs=3))
+        psum_2 = ctx.enter_context(tc.psum_pool(name="psum_2", bufs=3))
+        ctx.enter_context(tc.manual_schedule())
+
+        x_rows = {}
+
+        def load_x(g):
+            x_rows[g] = x_pool.tile([P, PACK * WIDTH], BF16, name="x_rows", tag="x_rows")
+            nc.sync.dma_start(out=x_rows[g][:], in_=x_groups[g])
+
+        w0_raw = consts.tile([P, PACK * WIDTH], BF16)
+        m0_raw = consts.tile([P, PACK * WIDTH], BF16)
+        w1_raw = consts.tile([P, PACK * WIDTH], BF16)
+        m1_raw = consts.tile([P, PACK * WIDTH], BF16)
+        b0_bf = consts.tile([P, PACK], BF16)
+        b1_bf = consts.tile([P, WIDTH], BF16)
+
+        load_x(0)
+        nc.sync.dma_start(out=w0_raw[:], in_=W0.rearrange("(m t) k -> m (t k)", t=PACK))
+        nc.sync.dma_start(out=m0_raw[:], in_=m0.rearrange("(m t) k -> m (t k)", t=PACK))
+        nc.sync.dma_start(out=b0_bf[:], in_=b0.rearrange("(m t) -> m t", t=PACK))
+        load_x(1)
+        nc.sync.dma_start(
+            out=w1_raw[:].rearrange("m (j k) -> m j k", j=PACK), in_=W1.rearrange("(j m) k -> m j k", m=P)
+        )
+        nc.sync.dma_start(
+            out=m1_raw[:].rearrange("m (j k) -> m j k", j=PACK), in_=m1.rearrange("(j m) k -> m j k", m=P)
+        )
+        nc.sync.dma_start(out=b1_bf[:], in_=b1.partition_broadcast(P))
+        for g in range(2, GROUPS):
+            load_x(g)
+
+        ident = consts.tile([P, P], F32)
+        make_identity(nc, ident[:])
+
+        def rows_onto_partitions(words, grouped):
+            grouped_words = grouped[:].bitcast(F32).rearrange("q (c u) -> q c u", u=2)
+            for half in range(2):
+                bank = psum_t.tile([P, 2, HALF], F32, name="bank", tag="bank")
+                for b in range(2):
+                    for u in range(2):
+                        nc.tensor.transpose(bank[:, u, b * P : (b + 1) * P], words[:, 2 * half + b, u, :], ident[:])
+                nc.scalar.copy(
+                    out=grouped_words[:, half * HALF : (half + 1) * HALF, :], in_=bank[:].rearrange("q u c -> q c u")
+                )
+
+        def mx_tiles(name):
+            codes = mx_pool.tile([P, WIDTH], U32, name=name + "_codes", tag=name + "_codes", align_bytes=64)
+            scales = mx_pool.tile([P, WIDTH], U8, name=name + "_scales", tag=name + "_scales", align_bytes=64)
+            return codes, scales
+
+        def masked_weight(raw, mask, word_order, name):
+            masked = consts.tile([P, PACK * WIDTH], BF16, name=name + "_masked")
+            nc.vector.tensor_tensor(out=masked[:], in0=raw[:], in1=mask[:], op=ALU.mult)
+            grouped = consts.tile([P, PACK * WIDTH], BF16, name=name + "_grouped", align_bytes=64)
+            rows_onto_partitions(masked[:].bitcast(F32).rearrange(word_order, b=PACK, u=2), grouped)
+            codes = consts.tile([P, WIDTH], U32, name=name + "_codes", align_bytes=64)
+            scales = consts.tile([P, WIDTH], U8, name=name + "_scales", align_bytes=64)
+            nc.vector.quantize_mx(out=codes[:].bitcast(FP8X4), scales=scales[:], in_=grouped[:])
+            return codes, scales
+
+        x_grouped = {}
+        x_mx = {}
+        h_planes = {}
+        h_mx = {}
+
+        def transpose_x(g):
+            x_grouped[g] = grouped_pool.tile(
+                [P, PACK * WIDTH], BF16, name="x_grouped", tag="x_grouped", align_bytes=64
+            )
+            rows_onto_partitions(
+                x_rows[g][:].bitcast(F32).rearrange("p (b u q) -> p b u q", b=PACK, u=2), x_grouped[g]
+            )
+
+        def quantise_x(g):
+            codes, scales = mx_tiles("x")
+            nc.vector.quantize_mx(out=codes[:].bitcast(FP8X4), scales=scales[:], in_=x_grouped[g][:])
+            x_mx[g] = (codes, scales)
+
+        def layer1(g):
+            codes, scales = x_mx[g]
+            h_planes[g] = grouped_pool.tile([P, PACK, WIDTH], BF16, name="h_planes", tag="h_planes")
+            for t in range(PACK):
+                acc = psum_1.tile([P, WIDTH], F32, name="acc1", tag="acc1")
+                nc.tensor.matmul_mx(
+                    out=acc[:],
+                    lhsT=w0_codes[:, t * P : (t + 1) * P].bitcast(FP8X4),
+                    lhsT_scale=w0_scales[:, t * P : (t + 1) * P],
+                    rhs=codes[:].bitcast(FP8X4),
+                    rhs_scale=scales[:],
+                    start=True,
+                    stop=True,
+                )
+                nc.scalar.activation(
+                    out=h_planes[g][:, t, :], in_=acc[:], func=ACT.Relu, bias=b0_f32[:, t : t + 1], scale=1.0
+                )
+
+        def quantise_h(g):
+            grouped = grouped_pool.tile([P, PACK * WIDTH], BF16, name="h_grouped", tag="h_grouped", align_bytes=64)
+            codes, scales = mx_tiles("h")
+            for half in range(2):
+                nc.vector.tensor_copy(
+                    out=grouped[:, half * PACK * HALF : (half + 1) * PACK * HALF].rearrange(
+                        "p (c i t) -> p c t i", i=4, t=PACK
+                    ),
+                    in_=h_planes[g][:, :, half * HALF : (half + 1) * HALF].rearrange("p t (c i) -> p c t i", i=4),
+                )
+            for half in range(2):
+                nc.vector.quantize_mx(
+                    out=codes[:, half * HALF : (half + 1) * HALF].bitcast(FP8X4),
+                    scales=scales[:, half * HALF : (half + 1) * HALF],
+                    in_=grouped[:, half * PACK * HALF : (half + 1) * PACK * HALF],
+                )
+            h_mx[g] = (codes, scales)
+
+        def layer2(g):
+            codes, scales = h_mx[g]
+            result = out_pool.tile([P, PACK, WIDTH], F32, name="result", tag="result")
+            for r in range(PACK):
+                acc = psum_2.tile([P, WIDTH], F32, name="acc2", tag="acc2")
+                nc.tensor.matmul_mx(
+                    out=acc[:],
+                    lhsT=codes[:, r * P : (r + 1) * P].bitcast(FP8X4),
+                    lhsT_scale=scales[:, r * P : (r + 1) * P],
+                    rhs=w1_codes[:].bitcast(FP8X4),
+                    rhs_scale=w1_scales[:],
+                    start=True,
+                    stop=True,
+                )
+                nc.vector.tensor_tensor(out=result[:, r, :], in0=acc[:], in1=b1_f32[:], op=ALU.add)
+                nc.gpsimd.tensor_scalar(
+                    out=result[:, r, :],
+                    in0=result[:, r, :],
+                    scalar1=FLOAT32_MAX,
+                    scalar2=0.0,
+                    op0=ALU.min,
+                    op1=ALU.max,
+                )
+            nc.sync.dma_start(out=out_groups[g], in_=result[:])
+
+        transpose_x(0)
+        w0_codes, w0_scales = masked_weight(w0_raw, m0_raw, "m (b u q) -> m b u q", "w0")
+        b0_f32 = consts.tile([P, PACK], F32)
+        nc.vector.tensor_copy(out=b0_f32[:], in_=b0_bf[:])
+        quantise_x(0)
+        layer1(0)
+        transpose_x(1)
+        w1_codes, w1_scales = masked_weight(w1_raw, m1_raw, "m (b q u) -> m b u q", "w1")
+        b1_f32 = consts.tile([P, WIDTH], F32)
+        nc.vector.tensor_copy(out=b1_f32[:], in_=b1_bf[:])
+        quantise_x(1)
+        layer1(1)
+        transpose_x(2)
+        for g in range(GROUPS):
+            if g + 3 < GROUPS:
+                transpose_x(g + 3)
+            quantise_h(g)
+            if g + 2 < GROUPS:
+                quantise_x(g + 2)
+            layer2(g)
+            if g + 2 < GROUPS:
+                layer1(g + 2)

@@ -17,7 +17,7 @@ WIDTH = P * PACK
 TOKENS = 8192
 GROUPS = TOKENS // WIDTH
 HALF = WIDTH // 2
-FLOAT32_MAX = 3.4028234663852886e38
+VECTOR_RELU_BLOCKS = 1
 
 FLOPS = 2 * 2 * TOKENS * WIDTH * WIDTH
 
@@ -99,6 +99,7 @@ def tile_patchedsparsenetwork_pa_t_kernel(tc, x, W0, b0, m0, W1, b1, m1, out):
         x_mx = {}
         h_planes = {}
         h_mx = {}
+        results = {}
 
         def transpose_x(g):
             x_grouped[g] = grouped_pool.tile(
@@ -164,15 +165,14 @@ def tile_patchedsparsenetwork_pa_t_kernel(tc, x, W0, b0, m0, W1, b1, m1, out):
                     stop=True,
                 )
                 nc.vector.tensor_tensor(out=result[:, r, :], in0=acc[:], in1=b1_f32[:], op=ALU.add)
-                nc.gpsimd.tensor_scalar(
-                    out=result[:, r, :],
-                    in0=result[:, r, :],
-                    scalar1=FLOAT32_MAX,
-                    scalar2=0.0,
-                    op0=ALU.min,
-                    op1=ALU.max,
-                )
-            nc.sync.dma_start(out=out_groups[g], in_=result[:])
+            results[g] = result
+
+        def relu_and_store(g):
+            on_vector = results[g][:, :VECTOR_RELU_BLOCKS, :]
+            on_scalar = results[g][:, VECTOR_RELU_BLOCKS:, :]
+            nc.vector.tensor_scalar_max(out=on_vector, in0=on_vector, scalar1=0.0)
+            nc.scalar.activation(out=on_scalar, in_=on_scalar, func=ACT.Relu)
+            nc.sync.dma_start(out=out_groups[g], in_=results[g][:])
 
         transpose_x(0)
         w0_codes, w0_scales = masked_weight(w0_raw, m0_raw, "m (b u q) -> m b u q", "w0")
@@ -190,9 +190,12 @@ def tile_patchedsparsenetwork_pa_t_kernel(tc, x, W0, b0, m0, W1, b1, m1, out):
         for g in range(GROUPS):
             if g + 3 < GROUPS:
                 transpose_x(g + 3)
+            if g >= 1:
+                relu_and_store(g - 1)
             quantise_h(g)
             if g + 2 < GROUPS:
                 quantise_x(g + 2)
             layer2(g)
             if g + 2 < GROUPS:
                 layer1(g + 2)
+        relu_and_store(GROUPS - 1)

@@ -17,7 +17,7 @@ WIDTH = P * PACK
 TOKENS = 8192
 GROUPS = TOKENS // WIDTH
 HALF = WIDTH // 2
-VECTOR_RELU_BLOCKS = 1
+FLOAT32_MAX = 3.4028234663852886e38
 
 FLOPS = 2 * 2 * TOKENS * WIDTH * WIDTH
 
@@ -31,7 +31,7 @@ def tile_patchedsparsenetwork_pa_t_kernel(tc, x, W0, b0, m0, W1, b1, m1, out):
         consts = ctx.enter_context(tc.tile_pool(name="consts", bufs=1))
         x_pool = ctx.enter_context(tc.tile_pool(name="x_pool", bufs=GROUPS))
         grouped_pool = ctx.enter_context(tc.tile_pool(name="grouped_pool", bufs=3))
-        mx_pool = ctx.enter_context(tc.tile_pool(name="mx_pool", bufs=2))
+        mx_pool = ctx.enter_context(tc.tile_pool(name="mx_pool", bufs=3))
         out_pool = ctx.enter_context(tc.tile_pool(name="out_pool", bufs=4))
         psum_t = ctx.enter_context(tc.psum_pool(name="psum_t", bufs=2))
         psum_1 = ctx.enter_context(tc.psum_pool(name="psum_1", bufs=3))
@@ -44,55 +44,73 @@ def tile_patchedsparsenetwork_pa_t_kernel(tc, x, W0, b0, m0, W1, b1, m1, out):
             x_rows[g] = x_pool.tile([P, PACK * WIDTH], BF16, name="x_rows", tag="x_rows")
             nc.sync.dma_start(out=x_rows[g][:], in_=x_groups[g])
 
-        w0_raw = consts.tile([P, PACK * WIDTH], BF16)
-        m0_raw = consts.tile([P, PACK * WIDTH], BF16)
-        w1_raw = consts.tile([P, PACK * WIDTH], BF16)
-        m1_raw = consts.tile([P, PACK * WIDTH], BF16)
+        def load_weight_and_mask(W, m, rows_of_partition, name):
+            raw = consts.tile([P, PACK * WIDTH], BF16, name=name + "_raw")
+            mask = consts.tile([P, PACK * WIDTH], BF16, name=name + "_mask")
+            for half in range(2):
+                for tile_, source in ((raw, W), (mask, m)):
+                    nc.sync.dma_start(
+                        out=tile_[:, half * PACK * HALF : (half + 1) * PACK * HALF].rearrange(
+                            "m (b k) -> m b k", k=WIDTH
+                        ),
+                        in_=source.rearrange(rows_of_partition, m=P)[:, half * PACK // 2 : (half + 1) * PACK // 2, :],
+                    )
+            return raw, mask
+
         b0_bf = consts.tile([P, PACK], BF16)
         b1_bf = consts.tile([P, WIDTH], BF16)
 
         load_x(0)
-        nc.sync.dma_start(out=w0_raw[:], in_=W0.rearrange("(m t) k -> m (t k)", t=PACK))
-        nc.sync.dma_start(out=m0_raw[:], in_=m0.rearrange("(m t) k -> m (t k)", t=PACK))
-        nc.sync.dma_start(out=b0_bf[:], in_=b0.rearrange("(m t) -> m t", t=PACK))
+        w0_raw, m0_raw = load_weight_and_mask(W0, m0, "(m t) k -> m t k", "w0")
         load_x(1)
-        nc.sync.dma_start(
-            out=w1_raw[:].rearrange("m (j k) -> m j k", j=PACK), in_=W1.rearrange("(j m) k -> m j k", m=P)
-        )
-        nc.sync.dma_start(
-            out=m1_raw[:].rearrange("m (j k) -> m j k", j=PACK), in_=m1.rearrange("(j m) k -> m j k", m=P)
-        )
+        nc.sync.dma_start(out=b0_bf[:], in_=b0.rearrange("(m t) -> m t", t=PACK))
+        w1_raw, m1_raw = load_weight_and_mask(W1, m1, "(j m) k -> m j k", "w1")
+        load_x(2)
         nc.sync.dma_start(out=b1_bf[:], in_=b1.partition_broadcast(P))
-        for g in range(2, GROUPS):
+        for g in range(3, GROUPS):
             load_x(g)
 
         ident = consts.tile([P, P], F32)
         make_identity(nc, ident[:])
 
-        def rows_onto_partitions(words, grouped):
+        def rows_onto_partitions(words, grouped, copy):
             grouped_words = grouped[:].bitcast(F32).rearrange("q (c u) -> q c u", u=2)
             for half in range(2):
                 bank = psum_t.tile([P, 2, HALF], F32, name="bank", tag="bank")
                 for b in range(2):
                     for u in range(2):
                         nc.tensor.transpose(bank[:, u, b * P : (b + 1) * P], words[:, 2 * half + b, u, :], ident[:])
-                nc.scalar.copy(
-                    out=grouped_words[:, half * HALF : (half + 1) * HALF, :], in_=bank[:].rearrange("q u c -> q c u")
+                copy(out=grouped_words[:, half * HALF : (half + 1) * HALF, :], in_=bank[:].rearrange("q u c -> q c u"))
+
+        def quantise_halves(grouped, codes, scales):
+            for half in range(2):
+                nc.vector.quantize_mx(
+                    out=codes[:, half * HALF : (half + 1) * HALF].bitcast(FP8X4),
+                    scales=scales[:, half * HALF : (half + 1) * HALF],
+                    in_=grouped[:, half * PACK * HALF : (half + 1) * PACK * HALF],
                 )
+
+        def mask_weight(raw, mask, name):
+            masked = consts.tile([P, PACK * WIDTH], BF16, name=name + "_masked")
+            for half in range(2):
+                cols = slice(half * PACK * HALF, (half + 1) * PACK * HALF)
+                nc.vector.tensor_tensor(out=masked[:, cols], in0=raw[:, cols], in1=mask[:, cols], op=ALU.mult)
+            return masked
+
+        def transpose_weight(masked, word_order, copy, name):
+            grouped = consts.tile([P, PACK * WIDTH], BF16, name=name + "_grouped", align_bytes=64)
+            rows_onto_partitions(masked[:].bitcast(F32).rearrange(word_order, b=PACK, u=2), grouped, copy)
+            return grouped
+
+        def quantise_weight(grouped, name):
+            codes = consts.tile([P, WIDTH], U32, name=name + "_codes", align_bytes=64)
+            scales = consts.tile([P, WIDTH], U8, name=name + "_scales", align_bytes=64)
+            quantise_halves(grouped, codes, scales)
+            return codes, scales
 
         def mx_tiles(name):
             codes = mx_pool.tile([P, WIDTH], U32, name=name + "_codes", tag=name + "_codes", align_bytes=64)
             scales = mx_pool.tile([P, WIDTH], U8, name=name + "_scales", tag=name + "_scales", align_bytes=64)
-            return codes, scales
-
-        def masked_weight(raw, mask, word_order, name):
-            masked = consts.tile([P, PACK * WIDTH], BF16, name=name + "_masked")
-            nc.vector.tensor_tensor(out=masked[:], in0=raw[:], in1=mask[:], op=ALU.mult)
-            grouped = consts.tile([P, PACK * WIDTH], BF16, name=name + "_grouped", align_bytes=64)
-            rows_onto_partitions(masked[:].bitcast(F32).rearrange(word_order, b=PACK, u=2), grouped)
-            codes = consts.tile([P, WIDTH], U32, name=name + "_codes", align_bytes=64)
-            scales = consts.tile([P, WIDTH], U8, name=name + "_scales", align_bytes=64)
-            nc.vector.quantize_mx(out=codes[:].bitcast(FP8X4), scales=scales[:], in_=grouped[:])
             return codes, scales
 
         x_grouped = {}
@@ -106,13 +124,13 @@ def tile_patchedsparsenetwork_pa_t_kernel(tc, x, W0, b0, m0, W1, b1, m1, out):
                 [P, PACK * WIDTH], BF16, name="x_grouped", tag="x_grouped", align_bytes=64
             )
             rows_onto_partitions(
-                x_rows[g][:].bitcast(F32).rearrange("p (b u q) -> p b u q", b=PACK, u=2), x_grouped[g]
+                x_rows[g][:].bitcast(F32).rearrange("p (b u q) -> p b u q", b=PACK, u=2), x_grouped[g], nc.scalar.copy
             )
 
         def quantise_x(g):
-            codes, scales = mx_tiles("x")
+            x_mx[g] = mx_tiles("x")
+            codes, scales = x_mx[g]
             nc.vector.quantize_mx(out=codes[:].bitcast(FP8X4), scales=scales[:], in_=x_grouped[g][:])
-            x_mx[g] = (codes, scales)
 
         def layer1(g):
             codes, scales = x_mx[g]
@@ -134,7 +152,6 @@ def tile_patchedsparsenetwork_pa_t_kernel(tc, x, W0, b0, m0, W1, b1, m1, out):
 
         def quantise_h(g):
             grouped = grouped_pool.tile([P, PACK * WIDTH], BF16, name="h_grouped", tag="h_grouped", align_bytes=64)
-            codes, scales = mx_tiles("h")
             for half in range(2):
                 nc.vector.tensor_copy(
                     out=grouped[:, half * PACK * HALF : (half + 1) * PACK * HALF].rearrange(
@@ -142,17 +159,12 @@ def tile_patchedsparsenetwork_pa_t_kernel(tc, x, W0, b0, m0, W1, b1, m1, out):
                     ),
                     in_=h_planes[g][:, :, half * HALF : (half + 1) * HALF].rearrange("p t (c i) -> p c t i", i=4),
                 )
-            for half in range(2):
-                nc.vector.quantize_mx(
-                    out=codes[:, half * HALF : (half + 1) * HALF].bitcast(FP8X4),
-                    scales=scales[:, half * HALF : (half + 1) * HALF],
-                    in_=grouped[:, half * PACK * HALF : (half + 1) * PACK * HALF],
-                )
-            h_mx[g] = (codes, scales)
+            h_mx[g] = mx_tiles("h")
+            quantise_halves(grouped, h_mx[g][0], h_mx[g][1])
 
         def layer2(g):
             codes, scales = h_mx[g]
-            result = out_pool.tile([P, PACK, WIDTH], F32, name="result", tag="result")
+            results[g] = out_pool.tile([P, PACK, WIDTH], F32, name="result", tag="result")
             for r in range(PACK):
                 acc = psum_2.tile([P, WIDTH], F32, name="acc2", tag="acc2")
                 nc.tensor.matmul_mx(
@@ -164,38 +176,53 @@ def tile_patchedsparsenetwork_pa_t_kernel(tc, x, W0, b0, m0, W1, b1, m1, out):
                     start=True,
                     stop=True,
                 )
-                nc.vector.tensor_tensor(out=result[:, r, :], in0=acc[:], in1=b1_f32[:], op=ALU.add)
-            results[g] = result
+                nc.vector.tensor_tensor(out=results[g][:, r, :], in0=acc[:], in1=b1_f32[:], op=ALU.add)
 
-        def relu_and_store(g):
-            on_vector = results[g][:, :VECTOR_RELU_BLOCKS, :]
-            on_scalar = results[g][:, VECTOR_RELU_BLOCKS:, :]
-            nc.vector.tensor_scalar_max(out=on_vector, in0=on_vector, scalar1=0.0)
-            nc.scalar.activation(out=on_scalar, in_=on_scalar, func=ACT.Relu)
-            nc.sync.dma_start(out=out_groups[g], in_=results[g][:])
+        def relu_first_half(g):
+            for r in range(PACK // 2):
+                nc.gpsimd.tensor_scalar(
+                    out=results[g][:, r, :],
+                    in0=results[g][:, r, :],
+                    scalar1=FLOAT32_MAX,
+                    scalar2=0.0,
+                    op0=ALU.min,
+                    op1=ALU.max,
+                )
+            nc.sync.dma_start(out=out_groups[g][:, : PACK // 2, :], in_=results[g][:, : PACK // 2, :])
+
+        def relu_second_half(g):
+            for r in range(PACK // 2, PACK):
+                nc.scalar.activation(out=results[g][:, r, :], in_=results[g][:, r, :], func=ACT.Relu)
+            nc.sync.dma_start(out=out_groups[g][:, PACK // 2 :, :], in_=results[g][:, PACK // 2 :, :])
 
         transpose_x(0)
-        w0_codes, w0_scales = masked_weight(w0_raw, m0_raw, "m (b u q) -> m b u q", "w0")
+        w0_masked = mask_weight(w0_raw, m0_raw, "w0")
+        quantise_x(0)
+        w0_grouped = transpose_weight(w0_masked, "m (b u q) -> m b u q", nc.scalar.copy, "w0")
+        w0_codes, w0_scales = quantise_weight(w0_grouped, "w0")
         b0_f32 = consts.tile([P, PACK], F32)
         nc.vector.tensor_copy(out=b0_f32[:], in_=b0_bf[:])
-        quantise_x(0)
-        layer1(0)
         transpose_x(1)
-        w1_codes, w1_scales = masked_weight(w1_raw, m1_raw, "m (b q u) -> m b u q", "w1")
+        layer1(0)
+        quantise_x(1)
+        w1_masked = mask_weight(w1_raw, m1_raw, "w1")
+        w1_grouped = transpose_weight(w1_masked, "m (b q u) -> m b u q", nc.vector.tensor_copy, "w1")
+        transpose_x(2)
+        layer1(1)
+        transpose_x(3)
+        quantise_h(0)
+        w1_codes, w1_scales = quantise_weight(w1_grouped, "w1")
         b1_f32 = consts.tile([P, WIDTH], F32)
         nc.vector.tensor_copy(out=b1_f32[:], in_=b1_bf[:])
-        quantise_x(1)
-        layer1(1)
-        transpose_x(2)
         for g in range(GROUPS):
-            if g + 3 < GROUPS:
-                transpose_x(g + 3)
-            if g >= 1:
-                relu_and_store(g - 1)
-            quantise_h(g)
             if g + 2 < GROUPS:
                 quantise_x(g + 2)
             layer2(g)
+            relu_first_half(g)
             if g + 2 < GROUPS:
                 layer1(g + 2)
-        relu_and_store(GROUPS - 1)
+            if g + 4 < GROUPS:
+                transpose_x(g + 4)
+            relu_second_half(g)
+            if g + 1 < GROUPS:
+                quantise_h(g + 1)

@@ -33,9 +33,8 @@ def tile_patchedsparsenetwork_pa_t_kernel(tc, x, W0, b0, m0, W1, b1, m1, out):
         grouped_pool = ctx.enter_context(tc.tile_pool(name="grouped_pool", bufs=3))
         mx_pool = ctx.enter_context(tc.tile_pool(name="mx_pool", bufs=3))
         out_pool = ctx.enter_context(tc.tile_pool(name="out_pool", bufs=4))
-        psum_t = ctx.enter_context(tc.psum_pool(name="psum_t", bufs=2))
-        psum_1 = ctx.enter_context(tc.psum_pool(name="psum_1", bufs=3))
-        psum_2 = ctx.enter_context(tc.psum_pool(name="psum_2", bufs=3))
+        psum_scalar = ctx.enter_context(tc.psum_pool(name="psum_scalar", bufs=4))
+        psum_vector = ctx.enter_context(tc.psum_pool(name="psum_vector", bufs=4))
         ctx.enter_context(tc.manual_schedule())
 
         x_rows = {}
@@ -73,14 +72,16 @@ def tile_patchedsparsenetwork_pa_t_kernel(tc, x, W0, b0, m0, W1, b1, m1, out):
         ident = consts.tile([P, P], F32)
         make_identity(nc, ident[:])
 
-        def rows_onto_partitions(words, grouped, copy):
+        def rows_onto_partitions(words, grouped):
             grouped_words = grouped[:].bitcast(F32).rearrange("q (c u) -> q c u", u=2)
             for half in range(2):
-                bank = psum_t.tile([P, 2, HALF], F32, name="bank", tag="bank")
+                bank = psum_scalar.tile([P, 2, HALF], F32, name="bank", tag="bank")
                 for b in range(2):
                     for u in range(2):
                         nc.tensor.transpose(bank[:, u, b * P : (b + 1) * P], words[:, 2 * half + b, u, :], ident[:])
-                copy(out=grouped_words[:, half * HALF : (half + 1) * HALF, :], in_=bank[:].rearrange("q u c -> q c u"))
+                nc.scalar.copy(
+                    out=grouped_words[:, half * HALF : (half + 1) * HALF, :], in_=bank[:].rearrange("q u c -> q c u")
+                )
 
         def quantise_halves(grouped, codes, scales):
             for half in range(2):
@@ -97,9 +98,9 @@ def tile_patchedsparsenetwork_pa_t_kernel(tc, x, W0, b0, m0, W1, b1, m1, out):
                 nc.vector.tensor_tensor(out=masked[:, cols], in0=raw[:, cols], in1=mask[:, cols], op=ALU.mult)
             return masked
 
-        def transpose_weight(masked, word_order, copy, name):
+        def transpose_weight(masked, word_order, name):
             grouped = consts.tile([P, PACK * WIDTH], BF16, name=name + "_grouped", align_bytes=64)
-            rows_onto_partitions(masked[:].bitcast(F32).rearrange(word_order, b=PACK, u=2), grouped, copy)
+            rows_onto_partitions(masked[:].bitcast(F32).rearrange(word_order, b=PACK, u=2), grouped)
             return grouped
 
         def quantise_weight(grouped, name):
@@ -116,6 +117,7 @@ def tile_patchedsparsenetwork_pa_t_kernel(tc, x, W0, b0, m0, W1, b1, m1, out):
         x_grouped = {}
         x_mx = {}
         h_planes = {}
+        h_grouped = {}
         h_mx = {}
         results = {}
 
@@ -124,7 +126,7 @@ def tile_patchedsparsenetwork_pa_t_kernel(tc, x, W0, b0, m0, W1, b1, m1, out):
                 [P, PACK * WIDTH], BF16, name="x_grouped", tag="x_grouped", align_bytes=64
             )
             rows_onto_partitions(
-                x_rows[g][:].bitcast(F32).rearrange("p (b u q) -> p b u q", b=PACK, u=2), x_grouped[g], nc.scalar.copy
+                x_rows[g][:].bitcast(F32).rearrange("p (b u q) -> p b u q", b=PACK, u=2), x_grouped[g]
             )
 
         def quantise_x(g):
@@ -136,7 +138,7 @@ def tile_patchedsparsenetwork_pa_t_kernel(tc, x, W0, b0, m0, W1, b1, m1, out):
             codes, scales = x_mx[g]
             h_planes[g] = grouped_pool.tile([P, PACK, WIDTH], BF16, name="h_planes", tag="h_planes")
             for t in range(PACK):
-                acc = psum_1.tile([P, WIDTH], F32, name="acc1", tag="acc1")
+                acc = psum_scalar.tile([P, WIDTH], F32, name="acc1", tag="bank")
                 nc.tensor.matmul_mx(
                     out=acc[:],
                     lhsT=w0_codes[:, t * P : (t + 1) * P].bitcast(FP8X4),
@@ -150,23 +152,24 @@ def tile_patchedsparsenetwork_pa_t_kernel(tc, x, W0, b0, m0, W1, b1, m1, out):
                     out=h_planes[g][:, t, :], in_=acc[:], func=ACT.Relu, bias=b0_f32[:, t : t + 1], scale=1.0
                 )
 
+        def regroup_h(g):
+            h_grouped[g] = grouped_pool.tile(
+                [P, PACK * WIDTH], BF16, name="h_grouped", tag="h_grouped", align_bytes=64
+            )
+            nc.vector.tensor_copy(
+                out=h_grouped[g][:].rearrange("p (c i t) -> p c t i", i=4, t=PACK),
+                in_=h_planes[g][:].rearrange("p t (c i) -> p c t i", i=4),
+            )
+
         def quantise_h(g):
-            grouped = grouped_pool.tile([P, PACK * WIDTH], BF16, name="h_grouped", tag="h_grouped", align_bytes=64)
-            for half in range(2):
-                nc.vector.tensor_copy(
-                    out=grouped[:, half * PACK * HALF : (half + 1) * PACK * HALF].rearrange(
-                        "p (c i t) -> p c t i", i=4, t=PACK
-                    ),
-                    in_=h_planes[g][:, :, half * HALF : (half + 1) * HALF].rearrange("p t (c i) -> p c t i", i=4),
-                )
             h_mx[g] = mx_tiles("h")
-            quantise_halves(grouped, h_mx[g][0], h_mx[g][1])
+            quantise_halves(h_grouped[g], h_mx[g][0], h_mx[g][1])
 
         def layer2(g):
             codes, scales = h_mx[g]
             results[g] = out_pool.tile([P, PACK, WIDTH], F32, name="result", tag="result")
             for r in range(PACK):
-                acc = psum_2.tile([P, WIDTH], F32, name="acc2", tag="acc2")
+                acc = psum_vector.tile([P, WIDTH], F32, name="acc2", tag="acc2")
                 nc.tensor.matmul_mx(
                     out=acc[:],
                     lhsT=codes[:, r * P : (r + 1) * P].bitcast(FP8X4),
@@ -198,25 +201,28 @@ def tile_patchedsparsenetwork_pa_t_kernel(tc, x, W0, b0, m0, W1, b1, m1, out):
         transpose_x(0)
         w0_masked = mask_weight(w0_raw, m0_raw, "w0")
         quantise_x(0)
-        w0_grouped = transpose_weight(w0_masked, "m (b u q) -> m b u q", nc.scalar.copy, "w0")
+        w0_grouped = transpose_weight(w0_masked, "m (b u q) -> m b u q", "w0")
         w0_codes, w0_scales = quantise_weight(w0_grouped, "w0")
         b0_f32 = consts.tile([P, PACK], F32)
         nc.vector.tensor_copy(out=b0_f32[:], in_=b0_bf[:])
         transpose_x(1)
         layer1(0)
-        quantise_x(1)
         w1_masked = mask_weight(w1_raw, m1_raw, "w1")
-        w1_grouped = transpose_weight(w1_masked, "m (b q u) -> m b u q", nc.vector.tensor_copy, "w1")
+        quantise_x(1)
+        w1_grouped = transpose_weight(w1_masked, "m (b q u) -> m b u q", "w1")
         transpose_x(2)
         layer1(1)
         transpose_x(3)
-        quantise_h(0)
+        regroup_h(0)
         w1_codes, w1_scales = quantise_weight(w1_grouped, "w1")
         b1_f32 = consts.tile([P, WIDTH], F32)
         nc.vector.tensor_copy(out=b1_f32[:], in_=b1_bf[:])
         for g in range(GROUPS):
+            quantise_h(g)
             if g + 2 < GROUPS:
                 quantise_x(g + 2)
+            if g + 1 < GROUPS:
+                regroup_h(g + 1)
             layer2(g)
             relu_first_half(g)
             if g + 2 < GROUPS:
@@ -224,5 +230,3 @@ def tile_patchedsparsenetwork_pa_t_kernel(tc, x, W0, b0, m0, W1, b1, m1, out):
             if g + 4 < GROUPS:
                 transpose_x(g + 4)
             relu_second_half(g)
-            if g + 1 < GROUPS:
-                quantise_h(g + 1)

@@ -181,22 +181,21 @@ def tile_patchedsparsenetwork_pa_t_kernel(tc, x, W0, b0, m0, W1, b1, m1, out):
                 )
                 nc.vector.tensor_tensor(out=results[g][:, r, :], in0=acc[:], in1=b1_f32[:], op=ALU.add)
 
-        def relu_first_half(g):
-            for r in range(PACK // 2):
-                nc.gpsimd.tensor_scalar(
-                    out=results[g][:, r, :],
-                    in0=results[g][:, r, :],
-                    scalar1=FLOAT32_MAX,
-                    scalar2=0.0,
-                    op0=ALU.min,
-                    op1=ALU.max,
-                )
-            nc.sync.dma_start(out=out_groups[g][:, : PACK // 2, :], in_=results[g][:, : PACK // 2, :])
+        def relu_on_gpsimd(g, r):
+            nc.gpsimd.tensor_scalar(
+                out=results[g][:, r, :],
+                in0=results[g][:, r, :],
+                scalar1=FLOAT32_MAX,
+                scalar2=0.0,
+                op0=ALU.min,
+                op1=ALU.max,
+            )
 
-        def relu_second_half(g):
-            for r in range(PACK // 2, PACK):
-                nc.scalar.activation(out=results[g][:, r, :], in_=results[g][:, r, :], func=ACT.Relu)
-            nc.sync.dma_start(out=out_groups[g][:, PACK // 2 :, :], in_=results[g][:, PACK // 2 :, :])
+        def relu_on_scalar(g, r):
+            nc.scalar.activation(out=results[g][:, r, :], in_=results[g][:, r, :], func=ACT.Relu)
+
+        def store(g, first, last):
+            nc.sync.dma_start(out=out_groups[g][:, first : last + 1, :], in_=results[g][:, first : last + 1, :])
 
         transpose_x(0)
         w0_masked = mask_weight(w0_raw, m0_raw, "w0")
@@ -224,9 +223,13 @@ def tile_patchedsparsenetwork_pa_t_kernel(tc, x, W0, b0, m0, W1, b1, m1, out):
             if g + 1 < GROUPS:
                 regroup_h(g + 1)
             layer2(g)
-            relu_first_half(g)
+            relu_on_gpsimd(g, 0)
+            relu_on_gpsimd(g, 3)
             if g + 2 < GROUPS:
                 layer1(g + 2)
             if g + 4 < GROUPS:
                 transpose_x(g + 4)
-            relu_second_half(g)
+            relu_on_scalar(g, 1)
+            relu_on_scalar(g, 2)
+            store(g, 0, 1)
+            store(g, 2, 3)

@@ -224,12 +224,12 @@ def tile_patchedsparsenetwork_pa_t_kernel(tc, x, W0, b0, m0, W1, b1, m1, out):
                 regroup_h(g + 1)
             layer2(g)
             relu_on_gpsimd(g, 0)
+            relu_on_gpsimd(g, 1)
             relu_on_gpsimd(g, 3)
             if g + 2 < GROUPS:
                 layer1(g + 2)
             if g + 4 < GROUPS:
                 transpose_x(g + 4)
-            relu_on_scalar(g, 1)
             relu_on_scalar(g, 2)
             store(g, 0, 1)
             store(g, 2, 3)

from contextlib import ExitStack

import concourse.mybir as mybir
from concourse.masks import make_identity

F32 = mybir.dt.float32
BF16 = mybir.dt.bfloat16
U32 = mybir.dt.uint32
U8 = mybir.dt.uint8
FP8X4 = mybir.dt.float8_e4m3fn_x4
ALU = mybir.AluOpType
ACT = mybir.ActivationFunctionType

P = 128
PACK = 4
WIDTH = P * PACK
TOKENS = 8192
GROUPS = TOKENS // WIDTH
HALF = WIDTH // 2
FLOAT32_MAX = 3.4028234663852886e38

FLOPS = 2 * 2 * TOKENS * WIDTH * WIDTH


def tile_patchedsparsenetwork_pa_t_kernel(tc, x, W0, b0, m0, W1, b1, m1, out):
    nc = tc.nc
    x_groups = x.rearrange("(g p r) k -> g p (r k)", p=P, r=PACK)
    out_groups = out.rearrange("(g p r) d -> g p r d", p=P, r=PACK)

    with ExitStack() as ctx:
        consts = ctx.enter_context(tc.tile_pool(name="consts", bufs=1))
        x_pool = ctx.enter_context(tc.tile_pool(name="x_pool", bufs=GROUPS))
        grouped_pool = ctx.enter_context(tc.tile_pool(name="grouped_pool", bufs=3))
        mx_pool = ctx.enter_context(tc.tile_pool(name="mx_pool", bufs=3))
        out_pool = ctx.enter_context(tc.tile_pool(name="out_pool", bufs=4))
        psum_scalar = ctx.enter_context(tc.psum_pool(name="psum_scalar", bufs=4))
        psum_vector = ctx.enter_context(tc.psum_pool(name="psum_vector", bufs=4))
        ctx.enter_context(tc.manual_schedule())

        x_rows = {}

        def load_x(g):
            x_rows[g] = x_pool.tile([P, PACK * WIDTH], BF16, name="x_rows", tag="x_rows")
            nc.sync.dma_start(out=x_rows[g][:], in_=x_groups[g])

        def load_weight_and_mask(W, m, rows_of_partition, name):
            raw = consts.tile([P, PACK * WIDTH], BF16, name=name + "_raw")
            mask = consts.tile([P, PACK * WIDTH], BF16, name=name + "_mask")
            for half in range(2):
                for tile_, source in ((raw, W), (mask, m)):
                    nc.sync.dma_start(
                        out=tile_[:, half * PACK * HALF : (half + 1) * PACK * HALF].rearrange(
                            "m (b k) -> m b k", k=WIDTH
                        ),
                        in_=source.rearrange(rows_of_partition, m=P)[:, half * PACK // 2 : (half + 1) * PACK // 2, :],
                    )
            return raw, mask

        b0_bf = consts.tile([P, PACK], BF16)
        b1_bf = consts.tile([P, WIDTH], BF16)

        load_x(0)
        w0_raw, m0_raw = load_weight_and_mask(W0, m0, "(m t) k -> m t k", "w0")
        load_x(1)
        nc.sync.dma_start(out=b0_bf[:], in_=b0.rearrange("(m t) -> m t", t=PACK))
        w1_raw, m1_raw = load_weight_and_mask(W1, m1, "(j m) k -> m j k", "w1")
        load_x(2)
        nc.sync.dma_start(out=b1_bf[:], in_=b1.partition_broadcast(P))
        for g in range(3, GROUPS):
            load_x(g)

        ident = consts.tile([P, P], F32)
        make_identity(nc, ident[:])

        def rows_onto_partitions(words, grouped):
            grouped_words = grouped[:].bitcast(F32).rearrange("q (c u) -> q c u", u=2)
            for half in range(2):
                bank = psum_scalar.tile([P, 2, HALF], F32, name="bank", tag="bank")
                for b in range(2):
                    for u in range(2):
                        nc.tensor.transpose(bank[:, u, b * P : (b + 1) * P], words[:, 2 * half + b, u, :], ident[:])
                nc.scalar.copy(
                    out=grouped_words[:, half * HALF : (half + 1) * HALF, :], in_=bank[:].rearrange("q u c -> q c u")
                )

        def quantise_halves(grouped, codes, scales):
            for half in range(2):
                nc.vector.quantize_mx(
                    out=codes[:, half * HALF : (half + 1) * HALF].bitcast(FP8X4),
                    scales=scales[:, half * HALF : (half + 1) * HALF],
                    in_=grouped[:, half * PACK * HALF : (half + 1) * PACK * HALF],
                )

        def mask_weight(raw, mask, name):
            masked = consts.tile([P, PACK * WIDTH], BF16, name=name + "_masked")
            for half in range(2):
                cols = slice(half * PACK * HALF, (half + 1) * PACK * HALF)
                nc.vector.tensor_tensor(out=masked[:, cols], in0=raw[:, cols], in1=mask[:, cols], op=ALU.mult)
            return masked

        def transpose_weight(masked, word_order, name):
            grouped = consts.tile([P, PACK * WIDTH], BF16, name=name + "_grouped", align_bytes=64)
            rows_onto_partitions(masked[:].bitcast(F32).rearrange(word_order, b=PACK, u=2), grouped)
            return grouped

        def quantise_weight(grouped, name):
            codes = consts.tile([P, WIDTH], U32, name=name + "_codes", align_bytes=64)
            scales = consts.tile([P, WIDTH], U8, name=name + "_scales", align_bytes=64)
            quantise_halves(grouped, codes, scales)
            return codes, scales

        def mx_tiles(name):
            codes = mx_pool.tile([P, WIDTH], U32, name=name + "_codes", tag=name + "_codes", align_bytes=64)
            scales = mx_pool.tile([P, WIDTH], U8, name=name + "_scales", tag=name + "_scales", align_bytes=64)
            return codes, scales

        x_grouped = {}
        x_mx = {}
        h_planes = {}
        h_grouped = {}
        h_mx = {}
        results = {}

        def transpose_x(g):
            x_grouped[g] = grouped_pool.tile(
                [P, PACK * WIDTH], BF16, name="x_grouped", tag="x_grouped", align_bytes=64
            )
            rows_onto_partitions(
                x_rows[g][:].bitcast(F32).rearrange("p (b u q) -> p b u q", b=PACK, u=2), x_grouped[g]
            )

        def quantise_x(g):
            x_mx[g] = mx_tiles("x")
            codes, scales = x_mx[g]
            nc.vector.quantize_mx(out=codes[:].bitcast(FP8X4), scales=scales[:], in_=x_grouped[g][:])

        def layer1(g):
            codes, scales = x_mx[g]
            h_planes[g] = grouped_pool.tile([P, PACK, WIDTH], BF16, name="h_planes", tag="h_planes")
            for t in range(PACK):
                acc = psum_scalar.tile([P, WIDTH], F32, name="acc1", tag="bank")
                nc.tensor.matmul_mx(
                    out=acc[:],
                    lhsT=w0_codes[:, t * P : (t + 1) * P].bitcast(FP8X4),
                    lhsT_scale=w0_scales[:, t * P : (t + 1) * P],
                    rhs=codes[:].bitcast(FP8X4),
                    rhs_scale=scales[:],
                    start=True,
                    stop=True,
                )
                nc.scalar.activation(
                    out=h_planes[g][:, t, :], in_=acc[:], func=ACT.Relu, bias=b0_f32[:, t : t + 1], scale=1.0
                )

        def regroup_h(g):
            h_grouped[g] = grouped_pool.tile(
                [P, PACK * WIDTH], BF16, name="h_grouped", tag="h_grouped", align_bytes=64
            )
            nc.vector.tensor_copy(
                out=h_grouped[g][:].rearrange("p (c i t) -> p c t i", i=4, t=PACK),
                in_=h_planes[g][:].rearrange("p t (c i) -> p c t i", i=4),
            )

        def quantise_h(g):
            h_mx[g] = mx_tiles("h")
            quantise_halves(h_grouped[g], h_mx[g][0], h_mx[g][1])

        def layer2(g):
            codes, scales = h_mx[g]
            results[g] = out_pool.tile([P, PACK, WIDTH], F32, name="result", tag="result")
            for r in range(PACK):
                acc = psum_vector.tile([P, WIDTH], F32, name="acc2", tag="acc2")
                nc.tensor.matmul_mx(
                    out=acc[:],
                    lhsT=codes[:, r * P : (r + 1) * P].bitcast(FP8X4),
                    lhsT_scale=scales[:, r * P : (r + 1) * P],
                    rhs=w1_codes[:].bitcast(FP8X4),
                    rhs_scale=w1_scales[:],
                    start=True,
                    stop=True,
                )
                nc.vector.tensor_tensor(out=results[g][:, r, :], in0=acc[:], in1=b1_f32[:], op=ALU.add)

        def relu_on_gpsimd(g, r):
            nc.gpsimd.tensor_scalar(
                out=results[g][:, r, :],
                in0=results[g][:, r, :],
                scalar1=FLOAT32_MAX,
                scalar2=0.0,
                op0=ALU.min,
                op1=ALU.max,
            )

        def relu_on_scalar(g, r):
            nc.scalar.activation(out=results[g][:, r, :], in_=results[g][:, r, :], func=ACT.Relu)

        def store(g, first, last):
            nc.sync.dma_start(out=out_groups[g][:, first : last + 1, :], in_=results[g][:, first : last + 1, :])

        transpose_x(0)
        w0_masked = mask_weight(w0_raw, m0_raw, "w0")
        quantise_x(0)
        w0_grouped = transpose_weight(w0_masked, "m (b u q) -> m b u q", "w0")
        w0_codes, w0_scales = quantise_weight(w0_grouped, "w0")
        b0_f32 = consts.tile([P, PACK], F32)
        nc.vector.tensor_copy(out=b0_f32[:], in_=b0_bf[:])
        transpose_x(1)
        layer1(0)
        w1_masked = mask_weight(w1_raw, m1_raw, "w1")
        quantise_x(1)
        w1_grouped = transpose_weight(w1_masked, "m (b q u) -> m b u q", "w1")
        transpose_x(2)
        layer1(1)
        transpose_x(3)
        regroup_h(0)
        w1_codes, w1_scales = quantise_weight(w1_grouped, "w1")
        b1_f32 = consts.tile([P, WIDTH], F32)
        nc.vector.tensor_copy(out=b1_f32[:], in_=b1_bf[:])
        for g in range(GROUPS):
            quantise_h(g)
            if g + 2 < GROUPS:
                quantise_x(g + 2)
            if g + 1 < GROUPS:
                regroup_h(g + 1)
            layer2(g)
            relu_on_gpsimd(g, 0)
            relu_on_gpsimd(g, 1)
            relu_on_gpsimd(g, 3)
            if g + 2 < GROUPS:
                layer1(g + 2)
            if g + 4 < GROUPS:
                transpose_x(g + 4)
            relu_on_scalar(g, 2)
            store(g, 0, 1)
            store(g, 2, 3)
